import numpy as np
import ml_dtypes


def mxq(x, axis, fmt="e4m3"):
    dtype, down = {"e4m3": (ml_dtypes.float8_e4m3fn, 7), "e5m2": (ml_dtypes.float8_e5m2, 14)}[fmt]
    v = np.moveaxis(np.asarray(x, np.float32).astype(ml_dtypes.bfloat16).astype(np.float64), axis, -1)
    blocks = v.reshape(v.shape[:-1] + (-1, 32))
    amax = np.abs(blocks).max(-1, keepdims=True)
    byte = np.maximum(np.where(amax > 0, np.frexp(amax)[1] - 1 + 127, 0) - down, 1)
    scale = np.exp2(byte - 127.0)
    codes = (blocks / scale).astype(np.float32).astype(dtype).astype(np.float64)
    return np.moveaxis((codes * scale).reshape(v.shape), -1, axis)


WIDE = False


def mx_kscale(k):
    if not WIDE:
        return np.ones(k)
    levels = np.array([10, -10, 5, -5, 0])
    if k % 512:
        return np.exp2(np.random.permutation(np.resize(levels, k // 32))).repeat(32)
    a = np.empty((k // 512, 16))
    for p in range(k // 512):
        a[p, :8] = np.random.permutation(np.resize(levels, 8))
        for g in range(8):
            far = levels[np.abs(levels - a[p, g]) >= 10]
            a[p, g + 8] = far[np.random.randint(len(far))]
    return np.exp2(a.ravel()).repeat(32)


BF16 = ml_dtypes.bfloat16


def bf(x):
    return np.asarray(x, np.float32).astype(BF16)


def f64(x):
    return np.asarray(x).astype(np.float64)


B, NT, N, C, DV, TM = 4, 128, 1024, 1024, 256, 128


def softmax(s):
    e = np.exp(s - s.max(-1, keepdims=True))
    return e / e.sum(-1, keepdims=True)


def setup_inputs():
    s = mx_kscale(C)
    q = np.random.standard_normal((B, 1, C)) + np.random.standard_normal((B, NT, C))
    k = bf(np.random.standard_normal((B, N, C)) * 1.4)
    ki = bf(np.random.standard_normal((B, N, C)) * 1.4)
    ki[-1] = k[-1]
    return {'q': bf(q), 'k': k, 'ki': ki,
            'xs': bf(np.random.standard_normal((B, N, C)) * s),
            'xis': bf(np.random.standard_normal((B, N, C)) * s),
            'Wv': bf(np.random.standard_normal((C, DV)) * 1.8 / np.sqrt(C) / s[:, None])}


def reference(q, k, ki, xs, xis, Wv):
    scale = C ** -0.5
    aw = softmax(f64(q) @ f64(k).transpose(0, 2, 1) * scale)
    awi = softmax(f64(q) @ f64(ki).transpose(0, 2, 1) * scale)
    D = aw - awi
    ones_cnt = np.where(D > 0, 1.0, 0.0).sum(axis=1)
    half_cnt = np.where(D == 0, 1.0, 0.0).sum(axis=1)
    rgb_ratio = (ones_cnt / NT)[..., None]
    eq_ratio = (half_cnt / NT)[..., None]
    tir_ratio = 1.0 - rgb_ratio - eq_ratio
    wv = mxq(f64(Wv), 0, 'e4m3')
    v = mxq(f64(xs), 2, 'e4m3') @ wv
    vi = mxq(f64(xis), 2, 'e4m3') @ wv
    return v * (rgb_ratio + eq_ratio) + vi * (tir_ratio + eq_ratio)

@@ -1,0 +1,421 @@
+from contextlib import ExitStack
+
+import concourse.masks as masks
+import concourse.mybir as mybir
+
+F32 = mybir.dt.float32
+BF16 = mybir.dt.bfloat16
+U32 = mybir.dt.uint32
+U8 = mybir.dt.uint8
+FP8X4 = mybir.dt.float8_e4m3fn_x4
+ALU = mybir.AluOpType
+ACTF = mybir.ActivationFunctionType
+AX = mybir.AxisListType
+
+B, NT, N, C, DV = 4, 128, 1024, 1024, 256
+P = 128
+FLOPS = 2 * 2 * B * NT * N * C + 2 * 2 * B * N * C * DV
+SCALE = 1.0 / 32.0
+
+MANUAL = True
+WEAVE = True
+NB = 8
+AHEAD = 7
+FIX = 60
+
+
+def tile_crossattention_for_fusion_temporal_pa_t_kernel(tc, q, k, ki, xs, xis, Wv, out):
+    nc = tc.nc
+    with ExitStack() as ctx:
+        if MANUAL:
+            ctx.enter_context(tc.manual_schedule())
+        const = ctx.enter_context(tc.tile_pool(name="const", bufs=1))
+        rawp = ctx.enter_context(tc.tile_pool(name="rawp", bufs=NB))
+        qp = ctx.enter_context(tc.tile_pool(name="qp", bufs=2))
+        ktp = ctx.enter_context(tc.tile_pool(name="ktp", bufs=4))
+        grpp = ctx.enter_context(tc.tile_pool(name="grpp", bufs=3))
+        codp = ctx.enter_context(tc.tile_pool(name="codp", bufs=4))
+        ep = ctx.enter_context(tc.tile_pool(name="ep", bufs=2))
+        stp = ctx.enter_context(tc.tile_pool(name="stp", bufs=4))
+        abp = ctx.enter_context(tc.tile_pool(name="abp", bufs=4))
+        outp = ctx.enter_context(tc.tile_pool(name="outp", bufs=3))
+        psum = ctx.enter_context(tc.psum_pool(name="psum", bufs=1))
+
+        ident = const.tile([P, P], F32, name="ident")
+        masks.make_identity(nc, ident[:])
+        ones = const.tile([P, 2], BF16, name="ones")
+        nc.vector.memset(ones[:], 1.0 / NT)
+
+        order = [("K", b, s, h) for b in range(B) for s in range(2) for h in range(2)]
+        order += [("X", b, s, h) for b in range(B) for h in range(2) for s in range(2)]
+        nstep = len(order)
+        NK = 16
+
+        srcs = {("K", 0): k, ("K", 1): ki, ("X", 0): xs, ("X", 1): xis}
+        raw = {}
+        qraw = {}
+        qT = {}
+        kT = {}
+        grp = {}
+        cod = {}
+        sca = {}
+        sps = {}
+        mx2 = {}
+        nbs = {}
+        ee = {}
+        z2 = {}
+        rz = {}
+        ind = {}
+        ab = {}
+        tmp = {}
+        osb = {}
+        wv = {}
+        st = {"v": 0, "s": 0, "mm": 0, "wb": 0, "sb": 0, "nwork": 5}
+
+        def work_bank(shape, name):
+            n = st["wb"] % st["nwork"]
+            st["wb"] += 1
+            return psum.tile(shape, F32, name=name, tag="bank%d" % n)
+
+        def score_bank():
+            n = 5 + st["sb"] % 3
+            st["sb"] += 1
+            return psum.tile([P, 512], F32, name="sacc", tag="bank%d" % n)
+
+        def charge(eng, cols):
+            st[eng] += cols + FIX
+
+        def copy_out(dst, src):
+            if st["v"] <= st["s"]:
+                charge("v", 512)
+                nc.vector.tensor_copy(out=dst, in_=src)
+            else:
+                charge("s", 512)
+                nc.scalar.copy(out=dst, in_=src)
+
+        def load_wv():
+            wr = const.tile([P, 2, 4, DV], BF16, name="wv_raw")
+            nc.sync.dma_start(
+                out=wr[:].rearrange("p g j d -> p g (j d)"),
+                in_=Wv.rearrange("(g p j) d -> p g (j d)", g=2, p=P, j=4),
+            )
+            wv["raw"] = wr
+
+        def prep_wv():
+            wr = wv["raw"]
+            wg = const.tile([P, 2, DV, 4], BF16, name="wv_grp", align_bytes=64)
+            for g in range(2):
+                nc.vector.tensor_copy(
+                    out=wg[:, g],
+                    in_=wr[:, g].rearrange("p j d -> p d j"),
+                )
+            wc = const.tile([P, 2 * DV], U32, name="wv_c", align_bytes=64)
+            ws = const.tile([P, 2 * DV], U8, name="wv_s", align_bytes=64)
+            nc.vector.quantize_mx(
+                out=wc[:].bitcast(FP8X4),
+                scales=ws[:],
+                in_=wg[:].rearrange("p g d j -> p (g d j)"),
+            )
+            wv["c"] = wc
+            wv["s"] = ws
+            charge("v", 1500)
+
+        def load_q(b):
+            qr = qp.tile([P, C], BF16, name="qraw", tag="qraw", bufs=4)
+            nc.sync.dma_start(out=qr[:], in_=q[b])
+            qraw[b] = qr
+
+        def load(i):
+            kind, b, s, h = order[i]
+            if i == 0:
+                load_q(0)
+            r = rawp.tile([P, 4, C], BF16, name="raw", tag="raw")
+            src = srcs[(kind, s)][b].rearrange("(p t) c -> p t c", t=8)
+            if i == 0:
+                for t in range(4):
+                    nc.sync.dma_start(out=r[:, t, :], in_=src[:, t, :])
+            else:
+                nc.sync.dma_start(out=r[:], in_=src[:, 4 * h : 4 * h + 4, :])
+            raw[i] = r
+            if kind == "K" and s == 0 and h == 0 and b + 1 < B:
+                load_q(b + 1)
+            if i == 9:
+                load_wv()
+
+        def q_transpose(b):
+            w = work_bank([P, 4, P], "wq")
+            qf = qraw[b][:].bitcast(F32)
+            for u in range(4):
+                nc.tensor.transpose(w[:, u, :], qf[:, P * u : P * (u + 1)], ident[:])
+            t = qp.tile([P, 4, 2, P], BF16, name="qT", tag="qT")
+            nc.vector.tensor_copy(
+                out=t[:],
+                in_=w[:].bitcast(BF16).rearrange("p u (n e) -> p u e n", e=2),
+            )
+            charge("v", 1024)
+            qT[b] = t
+
+        def score_mms(job):
+            kind, b, s, h = order[job]
+            acc = score_bank()
+            sps[(b, s, h)] = acc
+            kb = kT[job][:].bitcast(BF16).rearrange("p u (n e) -> p u n e", e=2)
+            return [(acc, qT[b], kb, u, e) for u in range(4) for e in range(2)]
+
+        def next_mm(mms):
+            if st["mm"] < len(mms):
+                acc, qt, kb, u, e = mms[st["mm"]]
+                st["mm"] += 1
+                nc.tensor.matmul(
+                    out=acc[:],
+                    lhsT=qt[:, u, e, :],
+                    rhs=kb[:, u, :, e],
+                    start=(u == 0 and e == 0),
+                    stop=(u == 3 and e == 1),
+                )
+
+        def transposes(i, mms, hook, last):
+            kind, b, s, h = order[i]
+            rf = raw[i][:].bitcast(F32)
+            if kind == "K":
+                dst = ktp.tile([P, 4, 512], F32, name="kT", tag="kT")
+                kT[i] = dst
+            else:
+                dst = grpp.tile([P, 4 * C], BF16, name="grp", tag="grp", align_bytes=64)
+                grp[i] = dst
+                dstf = dst[:].bitcast(F32).rearrange(
+                    "p (t g n u) -> p t g n u", t=4, g=2, n=P, u=2
+                )
+            for t in range(4):
+                w = work_bank([P, 4, P], "wt")
+                for u in range(4):
+                    if WEAVE and u % 2 == 0:
+                        next_mm(mms)
+                    if kind == "K":
+                        words = slice(P * u, P * (u + 1))
+                    else:
+                        words = slice(256 * (u // 2) + u % 2, 256 * (u // 2 + 1), 2)
+                    nc.tensor.transpose(w[:, u, :], rf[:, t, words], ident[:])
+                if hook and t == 0:
+                    st["s"] = min(st["s"], st["v"] - 1)
+                if kind == "K":
+                    copy_out(dst[:, :, P * t : P * (t + 1)], w[:])
+                else:
+                    copy_out(
+                        dstf[:, t], w[:].rearrange("p (g u) n -> p g n u", g=2, u=2)
+                    )
+                if hook and t == 0:
+                    exps(hook[0], hook[1])
+                if last and t == 1:
+                    quantise(i, 0, 2)
+
+        def quantise(i, part, parts):
+            if part == 0:
+                cod[i] = codp.tile([P, C], U32, name="cod", tag="cod", align_bytes=64)
+                sca[i] = codp.tile([P, C], U8, name="sca", tag="sca", align_bytes=64)
+            w = C // parts
+            cs = slice(part * w, (part + 1) * w)
+            nc.vector.quantize_mx(
+                out=cod[i][:, cs].bitcast(FP8X4),
+                scales=sca[i][:, cs],
+                in_=grp[i][:, 4 * part * w : 4 * (part + 1) * w],
+            )
+
+        def rowmax(b, s, h):
+            if h == 0:
+                mx2[(b, s)] = stp.tile([P, 2], F32, name="mx2", tag="mx2")
+            nc.vector.reduce_max(
+                out=mx2[(b, s)][:, h : h + 1], in_=sps[(b, s, h)][:], axis=AX.X
+            )
+
+        def negmax(b, s):
+            m = mx2[(b, s)]
+            nbt = stp.tile([P, 1], F32, name="nb", tag="nb")
+            nbs[(b, s)] = nbt
+            nc.vector.tensor_scalar(
+                out=nbt[:],
+                in0=m[:, 0:1],
+                scalar1=m[:, 1:2],
+                scalar2=-SCALE,
+                op0=ALU.max,
+                op1=ALU.mult,
+            )
+
+        def exps(b, s):
+            nbt = nbs[(b, s)]
+            e = ep.tile([P, N], F32, name="e%d" % s, tag="e%d" % s)
+            zz = stp.tile([P, 2], F32, name="z2", tag="z2")
+            for h in range(2):
+                nc.scalar.activation(
+                    out=e[:, 512 * h : 512 * (h + 1)],
+                    in_=sps[(b, s, h)][:],
+                    func=ACTF.Exp,
+                    bias=nbt[:, 0:1],
+                    scale=SCALE,
+                    accum_out=zz[:, h : h + 1],
+                )
+            ee[(b, s)] = e
+            z2[(b, s)] = zz
+
+        def compare(b, j):
+            o = ep.tile([P, N], BF16, name="ind%d" % j, tag="ind%d" % j)
+            nc.vector.scalar_tensor_tensor(
+                out=o[:],
+                in0=ee[(b, 0)][:],
+                scalar=rz[(b, 0)][:, 0:1],
+                in1=ee[(b, 1)][:],
+                op0=ALU.mult,
+                op1=(ALU.is_ge if j == 0 else ALU.is_le),
+            )
+            ind[(b, j)] = o
+
+        def votes_a(b):
+            for s in range(2):
+                zz = z2[(b, s)]
+                z = stp.tile([P, 1], F32, name="z", tag="z")
+                nc.vector.tensor_tensor(
+                    out=z[:], in0=zz[:, 0:1], in1=zz[:, 1:2], op=ALU.add
+                )
+                r = stp.tile([P, 1], F32, name="rz", tag="rz")
+                nc.vector.reciprocal(out=r[:], in_=z[:])
+                rz[(b, s)] = r
+            e1 = ee[(b, 1)]
+            nc.vector.tensor_scalar(
+                out=e1[:], in0=e1[:], scalar1=rz[(b, 1)][:, 0:1], scalar2=None, op0=ALU.mult
+            )
+            compare(b, 0)
+
+        def counts(b):
+            w = work_bank([P, 8, 2, 2], "wc")
+            for t in range(8):
+                for j in range(2):
+                    nc.tensor.matmul(
+                        out=w[:, t, j, :],
+                        lhsT=ind[(b, j)][:, P * t : P * (t + 1)],
+                        rhs=ones[:],
+                        start=True,
+                        stop=True,
+                    )
+            a = abp.tile([P, 8, 2, 2], F32, name="ab", tag="ab")
+            nc.vector.tensor_copy(out=a[:], in_=w[:])
+            ab[b] = a
+
+        def mx_bank(i, j, fine):
+            kind, b, s, h = order[i]
+            if j == 0:
+                if s == 0:
+                    tmp[(b, h)] = outp.tile([P, 4, DV], F32, name="tmp", tag="tmp")
+                else:
+                    osb[(b, h)] = outp.tile([P, 4, DV], F32, name="osb", tag="osb")
+            dst = tmp[(b, h)] if s == 0 else osb[(b, h)]
+            o = out[b].rearrange("(p t) d -> p t d", t=8)
+            if True:
+                w = work_bank([P, 2, DV], "wv")
+                for jj in range(2):
+                    t = 2 * j + jj
+                    for g in range(2):
+                        cs = slice((2 * t + g) * P, (2 * t + g + 1) * P)
+                        ws = slice(g * DV, (g + 1) * DV)
+                        nc.tensor.matmul_mx(
+                            out=w[:, jj, :],
+                            lhsT=cod[i][:, cs].bitcast(FP8X4),
+                            lhsT_scale=sca[i][:, cs],
+                            rhs=wv["c"][:, ws].bitcast(FP8X4),
+                            rhs_scale=wv["s"][:, ws],
+                            start=(g == 0),
+                            stop=(g == 1),
+                        )
+                for jj in range(2):
+                    t = 2 * j + jj
+                    gt = 4 * h + t
+                    if s == 0:
+                        nc.scalar.activation(
+                            out=dst[:, t, :],
+                            in_=w[:, jj, :],
+                            func=ACTF.Copy,
+                            scale=ab[b][:, gt, 0, 0:1],
+                        )
+                    else:
+                        nc.vector.scalar_tensor_tensor(
+                            out=dst[:, t, :],
+                            in0=w[:, jj, :],
+                            scalar=ab[b][:, gt, 1, 0:1],
+                            in1=tmp[(b, h)][:, t, :],
+                            op0=ALU.mult,
+                            op1=ALU.add,
+                        )
+                        if fine:
+                            nc.sync.dma_start(out=o[:, gt, :], in_=dst[:, t, :])
+            if s == 1 and j == 1 and not fine:
+                nc.sync.dma_start(out=o[:, 4 * h : 4 * h + 4, :], in_=dst[:])
+            if s == 1 and j == 0 and i == nstep - 1:
+                nc.sync.dma_start(out=o[:, 4 * h : 4 * h + 2, :], in_=dst[:, 0:2, :])
+
+        def mx_job(i):
+            mx_bank(i, 0, False)
+            mx_bank(i, 1, False)
+
+        for i in range(AHEAD):
+            load(i)
+        q_transpose(0)
+        for i in range(nstep):
+            if i + AHEAD < nstep:
+                load(i + AHEAD)
+            if i == 19:
+                st["nwork"] = 8
+                st["wb"] = 0
+            jq = i - 1
+            jr = i - 3
+            jm = i - 2
+            if NK <= jq < nstep:
+                charge("v", 1024)
+            if 0 <= jr < NK:
+                charge("v", 512)
+                if jr % 2 == 1:
+                    charge("v", 0)
+                    charge("s", 2 * 512 + 2 * FIX)
+            if 0 <= i - 7 < NK and (i - 7) % 4 == 0:
+                charge("v", 512 + 1024 + 6 * FIX)
+            if 0 <= i - 9 < NK and (i - 9) % 4 == 0:
+                charge("v", 1024)
+            if NK <= jm < nstep:
+                charge("s" if order[jm][2] == 0 else "v", 4 * (DV + FIX))
+
+            hook = None
+            if 0 <= jr < NK:
+                kind, b, s, h = order[jr]
+                rowmax(b, s, h)
+                if h == 1:
+                    negmax(b, s)
+                    hook = (b, s)
+            if i == 12:
+                prep_wv()
+            if NK <= jq < nstep:
+                quantise(jq, 0, 1)
+            if 0 <= i - 7 < NK and (i - 7) % 4 == 0:
+                votes_a((i - 7) // 4)
+            if 0 <= i - 9 < NK and (i - 9) % 4 == 0:
+                compare((i - 9) // 4, 1)
+            mms = []
+            st["mm"] = 0
+            if 0 <= i - 2 < NK:
+                mms = score_mms(i - 2)
+            if not WEAVE:
+                while st["mm"] < len(mms):
+                    next_mm(mms)
+            if i < nstep:
+                transposes(i, mms, hook, i == nstep - 1)
+            while st["mm"] < len(mms):
+                next_mm(mms)
+            if i < NK and i % 4 == 1 and i // 4 + 1 < B:
+                q_transpose(i // 4 + 1)
+            if 0 <= i - 10 < NK and (i - 10) % 4 == 0:
+                counts((i - 10) // 4)
+            if NK <= jm < nstep and i < nstep - 1:
+                mx_job(jm)
+        mx_bank(nstep - 3, 0, False)
+        quantise(nstep - 1, 1, 2)
+        mx_bank(nstep - 3, 1, False)
+        mx_job(nstep - 2)
+        mx_bank(nstep - 1, 0, False)
+        mx_bank(nstep - 1, 1, True)

@@ -32,12 +32,13 @@ def tile_crossattention_for_fusion_temporal_pa_t_kernel(tc, q, k, ki, xs, xis, W
         const = ctx.enter_context(tc.tile_pool(name="const", bufs=1))
         rawp = ctx.enter_context(tc.tile_pool(name="rawp", bufs=NB))
         qp = ctx.enter_context(tc.tile_pool(name="qp", bufs=2))
-        ktp = ctx.enter_context(tc.tile_pool(name="ktp", bufs=4))
+        ktp = ctx.enter_context(tc.tile_pool(name="ktp", bufs=3))
         grpp = ctx.enter_context(tc.tile_pool(name="grpp", bufs=3))
         codp = ctx.enter_context(tc.tile_pool(name="codp", bufs=4))
         ep = ctx.enter_context(tc.tile_pool(name="ep", bufs=2))
         stp = ctx.enter_context(tc.tile_pool(name="stp", bufs=4))
         abp = ctx.enter_context(tc.tile_pool(name="abp", bufs=4))
+        oddp = ctx.enter_context(tc.tile_pool(name="oddp", bufs=3))
         outp = ctx.enter_context(tc.tile_pool(name="outp", bufs=3))
         psum = ctx.enter_context(tc.psum_pool(name="psum", bufs=1))
 
@@ -56,6 +57,7 @@ def tile_crossattention_for_fusion_temporal_pa_t_kernel(tc, q, k, ki, xs, xis, W
         qraw = {}
         qT = {}
         kT = {}
+        odd = {}
         grp = {}
         cod = {}
         sca = {}
@@ -127,17 +129,17 @@ def tile_crossattention_for_fusion_temporal_pa_t_kernel(tc, q, k, ki, xs, xis, W
 
         def load(i):
             kind, b, s, h = order[i]
-            if i == 0:
-                load_q(0)
             r = rawp.tile([P, 4, C], BF16, name="raw", tag="raw")
             src = srcs[(kind, s)][b].rearrange("(p t) c -> p t c", t=8)
-            if i == 0:
+            if i < 3:
                 for t in range(4):
-                    nc.sync.dma_start(out=r[:, t, :], in_=src[:, t, :])
+                    nc.sync.dma_start(out=r[:, t, :], in_=src[:, 4 * h + t, :])
             else:
                 nc.sync.dma_start(out=r[:], in_=src[:, 4 * h : 4 * h + 4, :])
             raw[i] = r
-            if kind == "K" and s == 0 and h == 0 and b + 1 < B:
+            if i == 0:
+                load_q(0)
+            if kind == "K" and s == 0 and h == 1 and b + 1 < B:
                 load_q(b + 1)
             if i == 9:
                 load_wv()
@@ -174,9 +176,26 @@ def tile_crossattention_for_fusion_temporal_pa_t_kernel(tc, q, k, ki, xs, xis, W
                     stop=(u == 3 and e == 1),
                 )
 
+        def gather_odd(i):
+            odd[i] = oddp.tile([P, 4, 2, P], F32, name="odd", tag="odd")
+            src = raw[i][:].bitcast(F32).rearrange("p t (g w u) -> p t g w u", g=2, u=2)[:, :, :, :, 1]
+            if st["v"] + 512 <= st["s"] + 1024:
+                charge("v", 512)
+                nc.vector.tensor_copy(out=odd[i][:], in_=src)
+            else:
+                charge("s", 1024)
+                nc.scalar.copy(out=odd[i][:], in_=src)
+
+        def words_of(i, t, u):
+            rf = raw[i][:].bitcast(F32)
+            if order[i][0] == "K":
+                return rf[:, t, P * u : P * (u + 1)]
+            if u % 2 == 1:
+                return odd[i][:, t, u // 2, :]
+            return rf[:, t, 2 * P * (u // 2) : 2 * P * (u // 2 + 1) : 2]
+
         def transposes(i, mms, hook, last):
             kind, b, s, h = order[i]
-            rf = raw[i][:].bitcast(F32)
             if kind == "K":
                 dst = ktp.tile([P, 4, 512], F32, name="kT", tag="kT")
                 kT[i] = dst
@@ -191,11 +210,7 @@ def tile_crossattention_for_fusion_temporal_pa_t_kernel(tc, q, k, ki, xs, xis, W
                 for u in range(4):
                     if WEAVE and u % 2 == 0:
                         next_mm(mms)
-                    if kind == "K":
-                        words = slice(P * u, P * (u + 1))
-                    else:
-                        words = slice(256 * (u // 2) + u % 2, 256 * (u // 2 + 1), 2)
-                    nc.tensor.transpose(w[:, u, :], rf[:, t, words], ident[:])
+                    nc.tensor.transpose(w[:, u, :], words_of(i, t, u), ident[:])
                 if hook and t == 0:
                     st["s"] = min(st["s"], st["v"] - 1)
                 if kind == "K":
@@ -206,6 +221,12 @@ def tile_crossattention_for_fusion_temporal_pa_t_kernel(tc, q, k, ki, xs, xis, W
                     )
                 if hook and t == 0:
                     exps(hook[0], hook[1])
+                if t == 2 and NK <= i + 2 < nstep:
+                    gather_odd(i + 2)
+                if t == 1 and 0 <= i - 8 < NK and (i - 8) % 4 == 0:
+                    compare((i - 8) // 4, 0)
+                if t == 1 and 0 <= i - 9 < NK and (i - 9) % 4 == 0:
+                    compare((i - 9) // 4, 1)
                 if last and t == 1:
                     quantise(i, 0, 2)
 
@@ -283,7 +304,6 @@ def tile_crossattention_for_fusion_temporal_pa_t_kernel(tc, q, k, ki, xs, xis, W
             nc.vector.tensor_scalar(
                 out=e1[:], in0=e1[:], scalar1=rz[(b, 1)][:, 0:1], scalar2=None, op0=ALU.mult
             )
-            compare(b, 0)
 
         def counts(b):
             w = work_bank([P, 8, 2, 2], "wc")
@@ -357,7 +377,6 @@ def tile_crossattention_for_fusion_temporal_pa_t_kernel(tc, q, k, ki, xs, xis, W
 
         for i in range(AHEAD):
             load(i)
-        q_transpose(0)
         for i in range(nstep):
             if i + AHEAD < nstep:
                 load(i + AHEAD)
@@ -375,7 +394,9 @@ def tile_crossattention_for_fusion_temporal_pa_t_kernel(tc, q, k, ki, xs, xis, W
                     charge("v", 0)
                     charge("s", 2 * 512 + 2 * FIX)
             if 0 <= i - 7 < NK and (i - 7) % 4 == 0:
-                charge("v", 512 + 1024 + 6 * FIX)
+                charge("v", 512 + 5 * FIX)
+            if 0 <= i - 8 < NK and (i - 8) % 4 == 0:
+                charge("v", 1024)
             if 0 <= i - 9 < NK and (i - 9) % 4 == 0:
                 charge("v", 1024)
             if NK <= jm < nstep:
@@ -394,8 +415,6 @@ def tile_crossattention_for_fusion_temporal_pa_t_kernel(tc, q, k, ki, xs, xis, W
                 quantise(jq, 0, 1)
             if 0 <= i - 7 < NK and (i - 7) % 4 == 0:
                 votes_a((i - 7) // 4)
-            if 0 <= i - 9 < NK and (i - 9) % 4 == 0:
-                compare((i - 9) // 4, 1)
             mms = []
             st["mm"] = 0
             if 0 <= i - 2 < NK:
@@ -407,7 +426,9 @@ def tile_crossattention_for_fusion_temporal_pa_t_kernel(tc, q, k, ki, xs, xis, W
                 transposes(i, mms, hook, i == nstep - 1)
             while st["mm"] < len(mms):
                 next_mm(mms)
-            if i < NK and i % 4 == 1 and i // 4 + 1 < B:
+            if i == 0:
+                q_transpose(0)
+            if i < NK and i % 4 == 2 and i // 4 + 1 < B:
                 q_transpose(i // 4 + 1)
             if 0 <= i - 10 < NK and (i - 10) % 4 == 0:
                 counts((i - 10) // 4)

@@ -207,9 +207,10 @@ def tile_crossattention_for_fusion_temporal_pa_t_kernel(tc, q, k, ki, xs, xis, W
                 )
             for t in range(4):
                 w = work_bank([P, 4, P], "wt")
+                if WEAVE:
+                    next_mm(mms)
+                    next_mm(mms)
                 for u in range(4):
-                    if WEAVE and u % 2 == 0:
-                        next_mm(mms)
                     nc.tensor.transpose(w[:, u, :], words_of(i, t, u), ident[:])
                 if hook and t == 0:
                     st["s"] = min(st["s"], st["v"] - 1)

from contextlib import ExitStack

import concourse.masks as masks
import concourse.mybir as mybir

F32 = mybir.dt.float32
BF16 = mybir.dt.bfloat16
U32 = mybir.dt.uint32
U8 = mybir.dt.uint8
FP8X4 = mybir.dt.float8_e4m3fn_x4
ALU = mybir.AluOpType
ACTF = mybir.ActivationFunctionType
AX = mybir.AxisListType

B, NT, N, C, DV = 4, 128, 1024, 1024, 256
P = 128
FLOPS = 2 * 2 * B * NT * N * C + 2 * 2 * B * N * C * DV
SCALE = 1.0 / 32.0

MANUAL = True
WEAVE = True
NB = 8
AHEAD = 7
FIX = 60


def tile_crossattention_for_fusion_temporal_pa_t_kernel(tc, q, k, ki, xs, xis, Wv, out):
    nc = tc.nc
    with ExitStack() as ctx:
        if MANUAL:
            ctx.enter_context(tc.manual_schedule())
        const = ctx.enter_context(tc.tile_pool(name="const", bufs=1))
        rawp = ctx.enter_context(tc.tile_pool(name="rawp", bufs=NB))
        qp = ctx.enter_context(tc.tile_pool(name="qp", bufs=2))
        ktp = ctx.enter_context(tc.tile_pool(name="ktp", bufs=3))
        grpp = ctx.enter_context(tc.tile_pool(name="grpp", bufs=3))
        codp = ctx.enter_context(tc.tile_pool(name="codp", bufs=4))
        ep = ctx.enter_context(tc.tile_pool(name="ep", bufs=2))
        stp = ctx.enter_context(tc.tile_pool(name="stp", bufs=4))
        abp = ctx.enter_context(tc.tile_pool(name="abp", bufs=4))
        oddp = ctx.enter_context(tc.tile_pool(name="oddp", bufs=3))
        outp = ctx.enter_context(tc.tile_pool(name="outp", bufs=3))
        psum = ctx.enter_context(tc.psum_pool(name="psum", bufs=1))

        ident = const.tile([P, P], F32, name="ident")
        masks.make_identity(nc, ident[:])
        ones = const.tile([P, 2], BF16, name="ones")
        nc.vector.memset(ones[:], 1.0 / NT)

        order = [("K", b, s, h) for b in range(B) for s in range(2) for h in range(2)]
        order += [("X", b, s, h) for b in range(B) for h in range(2) for s in range(2)]
        nstep = len(order)
        NK = 16

        srcs = {("K", 0): k, ("K", 1): ki, ("X", 0): xs, ("X", 1): xis}
        raw = {}
        qraw = {}
        qT = {}
        kT = {}
        odd = {}
        grp = {}
        cod = {}
        sca = {}
        sps = {}
        mx2 = {}
        nbs = {}
        ee = {}
        z2 = {}
        rz = {}
        ind = {}
        ab = {}
        tmp = {}
        osb = {}
        wv = {}
        st = {"v": 0, "s": 0, "mm": 0, "wb": 0, "sb": 0, "nwork": 5}

        def work_bank(shape, name):
            n = st["wb"] % st["nwork"]
            st["wb"] += 1
            return psum.tile(shape, F32, name=name, tag="bank%d" % n)

        def score_bank():
            n = 5 + st["sb"] % 3
            st["sb"] += 1
            return psum.tile([P, 512], F32, name="sacc", tag="bank%d" % n)

        def charge(eng, cols):
            st[eng] += cols + FIX

        def copy_out(dst, src):
            if st["v"] <= st["s"]:
                charge("v", 512)
                nc.vector.tensor_copy(out=dst, in_=src)
            else:
                charge("s", 512)
                nc.scalar.copy(out=dst, in_=src)

        def load_wv():
            wr = const.tile([P, 2, 4, DV], BF16, name="wv_raw")
            nc.sync.dma_start(
                out=wr[:].rearrange("p g j d -> p g (j d)"),
                in_=Wv.rearrange("(g p j) d -> p g (j d)", g=2, p=P, j=4),
            )
            wv["raw"] = wr

        def prep_wv():
            wr = wv["raw"]
            wg = const.tile([P, 2, DV, 4], BF16, name="wv_grp", align_bytes=64)
            for g in range(2):
                nc.vector.tensor_copy(
                    out=wg[:, g],
                    in_=wr[:, g].rearrange("p j d -> p d j"),
                )
            wc = const.tile([P, 2 * DV], U32, name="wv_c", align_bytes=64)
            ws = const.tile([P, 2 * DV], U8, name="wv_s", align_bytes=64)
            nc.vector.quantize_mx(
                out=wc[:].bitcast(FP8X4),
                scales=ws[:],
                in_=wg[:].rearrange("p g d j -> p (g d j)"),
            )
            wv["c"] = wc
            wv["s"] = ws
            charge("v", 1500)

        def load_q(b):
            qr = qp.tile([P, C], BF16, name="qraw", tag="qraw", bufs=4)
            nc.sync.dma_start(out=qr[:], in_=q[b])
            qraw[b] = qr

        def load(i):
            kind, b, s, h = order[i]
            r = rawp.tile([P, 4, C], BF16, name="raw", tag="raw")
            src = srcs[(kind, s)][b].rearrange("(p t) c -> p t c", t=8)
            if i < 3:
                for t in range(4):
                    nc.sync.dma_start(out=r[:, t, :], in_=src[:, 4 * h + t, :])
            else:
                nc.sync.dma_start(out=r[:], in_=src[:, 4 * h : 4 * h + 4, :])
            raw[i] = r
            if i == 0:
                load_q(0)
            if kind == "K" and s == 0 and h == 1 and b + 1 < B:
                load_q(b + 1)
            if i == 9:
                load_wv()

        def q_transpose(b):
            w = work_bank([P, 4, P], "wq")
            qf = qraw[b][:].bitcast(F32)
            for u in range(4):
                nc.tensor.transpose(w[:, u, :], qf[:, P * u : P * (u + 1)], ident[:])
            t = qp.tile([P, 4, 2, P], BF16, name="qT", tag="qT")
            nc.vector.tensor_copy(
                out=t[:],
                in_=w[:].bitcast(BF16).rearrange("p u (n e) -> p u e n", e=2),
            )
            charge("v", 1024)
            qT[b] = t

        def score_mms(job):
            kind, b, s, h = order[job]
            acc = score_bank()
            sps[(b, s, h)] = acc
            kb = kT[job][:].bitcast(BF16).rearrange("p u (n e) -> p u n e", e=2)
            return [(acc, qT[b], kb, u, e) for u in range(4) for e in range(2)]

        def next_mm(mms):
            if st["mm"] < len(mms):
                acc, qt, kb, u, e = mms[st["mm"]]
                st["mm"] += 1
                nc.tensor.matmul(
                    out=acc[:],
                    lhsT=qt[:, u, e, :],
                    rhs=kb[:, u, :, e],
                    start=(u == 0 and e == 0),
                    stop=(u == 3 and e == 1),
                )

        def gather_odd(i):
            odd[i] = oddp.tile([P, 4, 2, P], F32, name="odd", tag="odd")
            src = raw[i][:].bitcast(F32).rearrange("p t (g w u) -> p t g w u", g=2, u=2)[:, :, :, :, 1]
            if st["v"] + 512 <= st["s"] + 1024:
                charge("v", 512)
                nc.vector.tensor_copy(out=odd[i][:], in_=src)
            else:
                charge("s", 1024)
                nc.scalar.copy(out=odd[i][:], in_=src)

        def words_of(i, t, u):
            rf = raw[i][:].bitcast(F32)
            if order[i][0] == "K":
                return rf[:, t, P * u : P * (u + 1)]
            if u % 2 == 1:
                return odd[i][:, t, u // 2, :]
            return rf[:, t, 2 * P * (u // 2) : 2 * P * (u // 2 + 1) : 2]

        def transposes(i, mms, hook, last):
            kind, b, s, h = order[i]
            if kind == "K":
                dst = ktp.tile([P, 4, 512], F32, name="kT", tag="kT")
                kT[i] = dst
            else:
                dst = grpp.tile([P, 4 * C], BF16, name="grp", tag="grp", align_bytes=64)
                grp[i] = dst
                dstf = dst[:].bitcast(F32).rearrange(
                    "p (t g n u) -> p t g n u", t=4, g=2, n=P, u=2
                )
            for t in range(4):
                w = work_bank([P, 4, P], "wt")
                if WEAVE:
                    next_mm(mms)
                    next_mm(mms)
                for u in range(4):
                    nc.tensor.transpose(w[:, u, :], words_of(i, t, u), ident[:])
                if hook and t == 0:
                    st["s"] = min(st["s"], st["v"] - 1)
                if kind == "K":
                    copy_out(dst[:, :, P * t : P * (t + 1)], w[:])
                else:
                    copy_out(
                        dstf[:, t], w[:].rearrange("p (g u) n -> p g n u", g=2, u=2)
                    )
                if hook and t == 0:
                    exps(hook[0], hook[1])
                if t == 2 and NK <= i + 2 < nstep:
                    gather_odd(i + 2)
                if t == 1 and 0 <= i - 8 < NK and (i - 8) % 4 == 0:
                    compare((i - 8) // 4, 0)
                if t == 1 and 0 <= i - 9 < NK and (i - 9) % 4 == 0:
                    compare((i - 9) // 4, 1)
                if last and t == 1:
                    quantise(i, 0, 2)

        def quantise(i, part, parts):
            if part == 0:
                cod[i] = codp.tile([P, C], U32, name="cod", tag="cod", align_bytes=64)
                sca[i] = codp.tile([P, C], U8, name="sca", tag="sca", align_bytes=64)
            w = C // parts
            cs = slice(part * w, (part + 1) * w)
            nc.vector.quantize_mx(
                out=cod[i][:, cs].bitcast(FP8X4),
                scales=sca[i][:, cs],
                in_=grp[i][:, 4 * part * w : 4 * (part + 1) * w],
            )

        def rowmax(b, s, h):
            if h == 0:
                mx2[(b, s)] = stp.tile([P, 2], F32, name="mx2", tag="mx2")
            nc.vector.reduce_max(
                out=mx2[(b, s)][:, h : h + 1], in_=sps[(b, s, h)][:], axis=AX.X
            )

        def negmax(b, s):
            m = mx2[(b, s)]
            nbt = stp.tile([P, 1], F32, name="nb", tag="nb")
            nbs[(b, s)] = nbt
            nc.vector.tensor_scalar(
                out=nbt[:],
                in0=m[:, 0:1],
                scalar1=m[:, 1:2],
                scalar2=-SCALE,
                op0=ALU.max,
                op1=ALU.mult,
            )

        def exps(b, s):
            nbt = nbs[(b, s)]
            e = ep.tile([P, N], F32, name="e%d" % s, tag="e%d" % s)
            zz = stp.tile([P, 2], F32, name="z2", tag="z2")
            for h in range(2):
                nc.scalar.activation(
                    out=e[:, 512 * h : 512 * (h + 1)],
                    in_=sps[(b, s, h)][:],
                    func=ACTF.Exp,
                    bias=nbt[:, 0:1],
                    scale=SCALE,
                    accum_out=zz[:, h : h + 1],
                )
            ee[(b, s)] = e
            z2[(b, s)] = zz

        def compare(b, j):
            o = ep.tile([P, N], BF16, name="ind%d" % j, tag="ind%d" % j)
            nc.vector.scalar_tensor_tensor(
                out=o[:],
                in0=ee[(b, 0)][:],
                scalar=rz[(b, 0)][:, 0:1],
                in1=ee[(b, 1)][:],
                op0=ALU.mult,
                op1=(ALU.is_ge if j == 0 else ALU.is_le),
            )
            ind[(b, j)] = o

        def votes_a(b):
            for s in range(2):
                zz = z2[(b, s)]
                z = stp.tile([P, 1], F32, name="z", tag="z")
                nc.vector.tensor_tensor(
                    out=z[:], in0=zz[:, 0:1], in1=zz[:, 1:2], op=ALU.add
                )
                r = stp.tile([P, 1], F32, name="rz", tag="rz")
                nc.vector.reciprocal(out=r[:], in_=z[:])
                rz[(b, s)] = r
            e1 = ee[(b, 1)]
            nc.vector.tensor_scalar(
                out=e1[:], in0=e1[:], scalar1=rz[(b, 1)][:, 0:1], scalar2=None, op0=ALU.mult
            )

        def counts(b):
            w = work_bank([P, 8, 2, 2], "wc")
            for t in range(8):
                for j in range(2):
                    nc.tensor.matmul(
                        out=w[:, t, j, :],
                        lhsT=ind[(b, j)][:, P * t : P * (t + 1)],
                        rhs=ones[:],
                        start=True,
                        stop=True,
                    )
            a = abp.tile([P, 8, 2, 2], F32, name="ab", tag="ab")
            nc.vector.tensor_copy(out=a[:], in_=w[:])
            ab[b] = a

        def mx_bank(i, j, fine):
            kind, b, s, h = order[i]
            if j == 0:
                if s == 0:
                    tmp[(b, h)] = outp.tile([P, 4, DV], F32, name="tmp", tag="tmp")
                else:
                    osb[(b, h)] = outp.tile([P, 4, DV], F32, name="osb", tag="osb")
            dst = tmp[(b, h)] if s == 0 else osb[(b, h)]
            o = out[b].rearrange("(p t) d -> p t d", t=8)
            if True:
                w = work_bank([P, 2, DV], "wv")
                for jj in range(2):
                    t = 2 * j + jj
                    for g in range(2):
                        cs = slice((2 * t + g) * P, (2 * t + g + 1) * P)
                        ws = slice(g * DV, (g + 1) * DV)
                        nc.tensor.matmul_mx(
                            out=w[:, jj, :],
                            lhsT=cod[i][:, cs].bitcast(FP8X4),
                            lhsT_scale=sca[i][:, cs],
                            rhs=wv["c"][:, ws].bitcast(FP8X4),
                            rhs_scale=wv["s"][:, ws],
                            start=(g == 0),
                            stop=(g == 1),
                        )
                for jj in range(2):
                    t = 2 * j + jj
                    gt = 4 * h + t
                    if s == 0:
                        nc.scalar.activation(
                            out=dst[:, t, :],
                            in_=w[:, jj, :],
                            func=ACTF.Copy,
                            scale=ab[b][:, gt, 0, 0:1],
                        )
                    else:
                        nc.vector.scalar_tensor_tensor(
                            out=dst[:, t, :],
                            in0=w[:, jj, :],
                            scalar=ab[b][:, gt, 1, 0:1],
                            in1=tmp[(b, h)][:, t, :],
                            op0=ALU.mult,
                            op1=ALU.add,
                        )
                        if fine:
                            nc.sync.dma_start(out=o[:, gt, :], in_=dst[:, t, :])
            if s == 1 and j == 1 and not fine:
                nc.sync.dma_start(out=o[:, 4 * h : 4 * h + 4, :], in_=dst[:])
            if s == 1 and j == 0 and i == nstep - 1:
                nc.sync.dma_start(out=o[:, 4 * h : 4 * h + 2, :], in_=dst[:, 0:2, :])

        def mx_job(i):
            mx_bank(i, 0, False)
            mx_bank(i, 1, False)

        for i in range(AHEAD):
            load(i)
        for i in range(nstep):
            if i + AHEAD < nstep:
                load(i + AHEAD)
            if i == 19:
                st["nwork"] = 8
                st["wb"] = 0
            jq = i - 1
            jr = i - 3
            jm = i - 2
            if NK <= jq < nstep:
                charge("v", 1024)
            if 0 <= jr < NK:
                charge("v", 512)
                if jr % 2 == 1:
                    charge("v", 0)
                    charge("s", 2 * 512 + 2 * FIX)
            if 0 <= i - 7 < NK and (i - 7) % 4 == 0:
                charge("v", 512 + 5 * FIX)
            if 0 <= i - 8 < NK and (i - 8) % 4 == 0:
                charge("v", 1024)
            if 0 <= i - 9 < NK and (i - 9) % 4 == 0:
                charge("v", 1024)
            if NK <= jm < nstep:
                charge("s" if order[jm][2] == 0 else "v", 4 * (DV + FIX))

            hook = None
            if 0 <= jr < NK:
                kind, b, s, h = order[jr]
                rowmax(b, s, h)
                if h == 1:
                    negmax(b, s)
                    hook = (b, s)
            if i == 12:
                prep_wv()
            if NK <= jq < nstep:
                quantise(jq, 0, 1)
            if 0 <= i - 7 < NK and (i - 7) % 4 == 0:
                votes_a((i - 7) // 4)
            mms = []
            st["mm"] = 0
            if 0 <= i - 2 < NK:
                mms = score_mms(i - 2)
            if not WEAVE:
                while st["mm"] < len(mms):
                    next_mm(mms)
            if i < nstep:
                transposes(i, mms, hook, i == nstep - 1)
            while st["mm"] < len(mms):
                next_mm(mms)
            if i == 0:
                q_transpose(0)
            if i < NK and i % 4 == 2 and i // 4 + 1 < B:
                q_transpose(i // 4 + 1)
            if 0 <= i - 10 < NK and (i - 10) % 4 == 0:
                counts((i - 10) // 4)
            if NK <= jm < nstep and i < nstep - 1:
                mx_job(jm)
        mx_bank(nstep - 3, 0, False)
        quantise(nstep - 1, 1, 2)
        mx_bank(nstep - 3, 1, False)
        mx_job(nstep - 2)
        mx_bank(nstep - 1, 0, False)
        mx_bank(nstep - 1, 1, True)
